import numpy as np
import ml_dtypes


def mxq(x, axis, fmt="e4m3"):
    dtype, down = {"e4m3": (ml_dtypes.float8_e4m3fn, 7), "e5m2": (ml_dtypes.float8_e5m2, 14)}[fmt]
    v = np.moveaxis(np.asarray(x, np.float32).astype(ml_dtypes.bfloat16).astype(np.float64), axis, -1)
    blocks = v.reshape(v.shape[:-1] + (-1, 32))
    amax = np.abs(blocks).max(-1, keepdims=True)
    byte = np.maximum(np.where(amax > 0, np.frexp(amax)[1] - 1 + 127, 0) - down, 1)
    scale = np.exp2(byte - 127.0)
    codes = (blocks / scale).astype(np.float32).astype(dtype).astype(np.float64)
    return np.moveaxis((codes * scale).reshape(v.shape), -1, axis)


WIDE = False


def mx_kscale(k):
    if not WIDE:
        return np.ones(k)
    levels = np.array([10, -10, 5, -5, 0])
    if k % 512:
        return np.exp2(np.random.permutation(np.resize(levels, k // 32))).repeat(32)
    a = np.empty((k // 512, 16))
    for p in range(k // 512):
        a[p, :8] = np.random.permutation(np.resize(levels, 8))
        for g in range(8):
            far = levels[np.abs(levels - a[p, g]) >= 10]
            a[p, g + 8] = far[np.random.randint(len(far))]
    return np.exp2(a.ravel()).repeat(32)


BF16 = ml_dtypes.bfloat16


def bf(x):
    return np.asarray(x, np.float32).astype(BF16)


def f64(x):
    return np.asarray(x).astype(np.float64)


BATCH, IN_F, OUT_F, RANK, N_ADAPTERS = 1024, 16384, 128, 128, 8
SEG = BATCH // N_ADAPTERS
LORA_GAIN = 2.0


def setup_inputs():
    s = mx_kscale(IN_F)
    return {"x": bf(np.random.standard_normal((BATCH, IN_F)) * s),
            "h_lora": bf(np.random.standard_normal((N_ADAPTERS, SEG, RANK))),
            "lora_B": bf(np.random.standard_normal((N_ADAPTERS, RANK, OUT_F)) * 0.5 / np.sqrt(RANK)),
            "M": bf(np.random.standard_normal((IN_F, OUT_F)) / np.sqrt(IN_F) / s[:, None])}


def reference(x, h_lora, lora_B, M):
    y = (f64(h_lora) @ f64(lora_B)) * LORA_GAIN
    y = y.reshape(BATCH, OUT_F)
    return y + (mxq(f64(x), 1, "e4m3") @ mxq(f64(M), 0, "e4m3"))

@@ -1,0 +1,198 @@
+from contextlib import ExitStack
+
+import concourse.mybir as mybir
+from concourse.masks import make_identity
+
+BF16 = mybir.dt.bfloat16
+F32 = mybir.dt.float32
+U32 = mybir.dt.uint32
+U8 = mybir.dt.uint8
+FP8X4 = mybir.dt.float8_e4m3fn_x4
+ADD = mybir.AluOpType.add
+
+P = 128
+BATCH, IN_F, OUT_F, RANK, N_ADAPTERS = 1024, 16384, 128, 128, 8
+LORA_GAIN = 2.0
+
+PACK = 4
+K_PASS = P * PACK
+CHUNK_K = 4096
+PASSES = CHUNK_K // K_PASS
+K_STEPS = IN_F // CHUNK_K
+ROW_TILES = BATCH // P
+N_CHUNKS = K_STEPS * ROW_TILES
+BANK_PASSES = 2
+CHUNK_BANKS = PASSES // BANK_PASSES
+QUANT_COLS = 2048
+
+LOADS_AHEAD = 6
+QUANTISE_LAG = 1
+MULTIPLY_LAG = 2
+M_GROUP = 2
+M_ROUNDS = PASSES // M_GROUP
+VECTOR_BANK_EVERY = 8
+
+FLOPS = 2 * BATCH * IN_F * OUT_F + 2 * BATCH * RANK * OUT_F
+
+
+def tile_lorasequential_pa_k_kernel(tc, x, h_lora, lora_B, M, out):
+    nc = tc.nc
+    with ExitStack() as ctx:
+        ctx.enter_context(tc.manual_schedule())
+        const = ctx.enter_context(tc.tile_pool(name="const", bufs=1))
+        x_pool = ctx.enter_context(tc.tile_pool(name="x", bufs=LOADS_AHEAD + 1))
+        x_mx_pool = ctx.enter_context(tc.tile_pool(name="x_mx", bufs=3))
+        m_raw_pool = ctx.enter_context(tc.tile_pool(name="m_raw", bufs=2))
+        m_grouped_pool = ctx.enter_context(tc.tile_pool(name="m_grouped", bufs=3))
+        m_mx_pool = ctx.enter_context(tc.tile_pool(name="m_mx", bufs=2))
+        result_pool = ctx.enter_context(tc.tile_pool(name="result", bufs=4))
+        psum_t = ctx.enter_context(tc.psum_pool(name="psum_t", bufs=6))
+        psum_acc = ctx.enter_context(tc.psum_pool(name="psum_acc", bufs=2))
+
+        ident_f32 = const.tile([P, P], F32)
+        make_identity(nc, ident_f32[:])
+        ident_bf16 = const.tile([P, P], BF16)
+        make_identity(nc, ident_bf16[:])
+
+        x_raw = {}
+        x_grouped = {}
+        x_codes = {}
+        x_scales = {}
+        m_raw = {}
+        m_grouped = {}
+        m_codes = {}
+        m_scales = {}
+
+        def load_m(step):
+            raw = m_raw_pool.tile([P, PASSES, PACK, OUT_F], BF16, name="m_raw")
+            m_rows = M[step * CHUNK_K : (step + 1) * CHUNK_K, :]
+            nc.sync.dma_start(
+                out=raw[:],
+                in_=m_rows.rearrange("(g p t) o -> p g t o", p=P, t=PACK),
+            )
+            m_raw[step] = raw
+
+        def load_x(chunk):
+            step, row_tile = divmod(chunk, ROW_TILES)
+            if row_tile == ROW_TILES - MULTIPLY_LAG and step + 1 < K_STEPS:
+                load_m(step + 1)
+            raw = x_pool.tile([P, CHUNK_K], BF16, name="x_raw")
+            x_rows = x[row_tile * P : (row_tile + 1) * P, step * CHUNK_K : (step + 1) * CHUNK_K]
+            pieces = CHUNK_BANKS if chunk == N_CHUNKS - 1 else 1
+            piece_k = CHUNK_K // pieces
+            for first in range(0, CHUNK_K, piece_k):
+                nc.sync.dma_start(out=raw[:, first : first + piece_k], in_=x_rows[:, first : first + piece_k])
+            x_raw[chunk] = raw
+
+        def regroup_m(step, j):
+            grouped = m_grouped_pool.tile([P, M_GROUP, OUT_F, PACK], BF16, name="m_grouped", align_bytes=64)
+            nc.vector.tensor_copy(
+                out=grouped[:],
+                in_=m_raw[step][:, j * M_GROUP : (j + 1) * M_GROUP, :, :].rearrange("p g t o -> p g o t"),
+            )
+            m_grouped[step, j] = grouped
+
+        def quantise_m(step, j):
+            if j == 0:
+                m_codes[step] = m_mx_pool.tile([P, PASSES * OUT_F], U32, name="m_codes", align_bytes=64)
+                m_scales[step] = m_mx_pool.tile([P, PASSES * OUT_F], U8, name="m_scales", align_bytes=64)
+            cols = slice(j * M_GROUP * OUT_F, (j + 1) * M_GROUP * OUT_F)
+            nc.vector.quantize_mx(
+                out=m_codes[step][:, cols].bitcast(FP8X4),
+                scales=m_scales[step][:, cols],
+                in_=m_grouped[step, j][:].rearrange("p g o t -> p (g o t)"),
+            )
+
+        def transpose_x(chunk):
+            words = x_raw[chunk][:].bitcast(F32)
+            grouped = x_mx_pool.tile([P, PASSES * P * PACK], BF16, name="x_grouped", align_bytes=64)
+            grouped_words = grouped[:].bitcast(F32)
+            bank_words = BANK_PASSES * P * 2
+            for bank in range(CHUNK_BANKS):
+                xt = psum_t.tile([P, BANK_PASSES, 2, P], F32, name="xt", tag="bank")
+                for g in range(BANK_PASSES):
+                    first = (bank * BANK_PASSES + g) * 2 * P
+                    for u in range(2):
+                        nc.tensor.transpose(xt[:, g, u, :], words[:, first + u : first + 2 * P : 2], ident_f32[:])
+                side_by_side = grouped_words[:, bank * bank_words : (bank + 1) * bank_words].rearrange(
+                    "p (g r u) -> p g r u", g=BANK_PASSES, u=2
+                )
+                if (chunk * CHUNK_BANKS + bank) % VECTOR_BANK_EVERY == VECTOR_BANK_EVERY - 1:
+                    nc.vector.tensor_copy(out=side_by_side, in_=xt[:].rearrange("p g u r -> p g r u"))
+                else:
+                    nc.scalar.copy(out=side_by_side, in_=xt[:].rearrange("p g u r -> p g r u"))
+            x_grouped[chunk] = grouped
+
+        def quantise_x(chunk):
+            codes = x_mx_pool.tile([P, PASSES * P], U32, name="x_codes", align_bytes=64)
+            scales = x_mx_pool.tile([P, PASSES * P], U8, name="x_scales", align_bytes=64)
+            for first in range(0, PASSES * P * PACK, QUANT_COLS):
+                cols = slice(first // PACK, (first + QUANT_COLS) // PACK)
+                nc.vector.quantize_mx(
+                    out=codes[:, cols].bitcast(FP8X4),
+                    scales=scales[:, cols],
+                    in_=x_grouped[chunk][:, first : first + QUANT_COLS],
+                )
+            x_codes[chunk] = codes
+            x_scales[chunk] = scales
+
+        def multiply(chunk):
+            step, row_tile = divmod(chunk, ROW_TILES)
+            acc = psum_acc.tile([P, OUT_F], F32, name="acc")
+            for g in range(PASSES):
+                rows = slice(g * P, (g + 1) * P)
+                outputs = slice(g * OUT_F, (g + 1) * OUT_F)
+                nc.tensor.matmul_mx(
+                    out=acc[:],
+                    lhsT=x_codes[chunk][:, rows].bitcast(FP8X4),
+                    lhsT_scale=x_scales[chunk][:, rows],
+                    rhs=m_codes[step][:, outputs].bitcast(FP8X4),
+                    rhs_scale=m_scales[step][:, outputs],
+                    start=(g == 0),
+                    stop=(g == PASSES - 1),
+                )
+            if step < K_STEPS - 1:
+                nc.vector.tensor_tensor(out=sums[:, row_tile, :], in0=acc[:], in1=sums[:, row_tile, :], op=ADD)
+            else:
+                result = result_pool.tile([P, OUT_F], F32, name="result")
+                nc.vector.tensor_tensor(out=result[:], in0=acc[:], in1=sums[:, row_tile, :], op=ADD)
+                nc.sync.dma_start(out=out[row_tile * P : (row_tile + 1) * P, :], in_=result[:])
+
+        h_sb = const.tile([P, N_ADAPTERS, RANK], BF16)
+        nc.sync.dma_start(out=h_sb[:], in_=h_lora.rearrange("g b r -> b g r"))
+        b_sb = const.tile([P, N_ADAPTERS, OUT_F], BF16)
+        nc.sync.dma_start(out=b_sb[:], in_=lora_B.rearrange("g r o -> r g o"))
+        load_m(0)
+        for chunk in range(LOADS_AHEAD):
+            load_x(chunk)
+
+        sums = const.tile([P, ROW_TILES, OUT_F], F32)
+        hT_ps = psum_t.tile([P, N_ADAPTERS, P], BF16, name="hT_ps", tag="bank")
+        for g in range(N_ADAPTERS):
+            nc.tensor.transpose(hT_ps[:, g, :], h_sb[:, g, :], ident_bf16[:])
+        hT_sb = const.tile([P, N_ADAPTERS, P], BF16)
+        nc.scalar.copy(out=hT_sb[:], in_=hT_ps[:])
+        bank_groups = 4
+        for first in range(0, N_ADAPTERS, bank_groups):
+            y_ps = psum_t.tile([P, bank_groups, OUT_F], F32, name="y_ps", tag="bank")
+            for g in range(bank_groups):
+                nc.tensor.matmul(
+                    y_ps[:, g, :], lhsT=hT_sb[:, first + g, :], rhs=b_sb[:, first + g, :], start=True, stop=True
+                )
+            nc.scalar.mul(out=sums[:, first : first + bank_groups, :], in_=y_ps[:], mul=LORA_GAIN)
+
+        for i in range(-MULTIPLY_LAG, N_CHUNKS + MULTIPLY_LAG):
+            if 0 <= i and i + LOADS_AHEAD < N_CHUNKS:
+                load_x(i + LOADS_AHEAD)
+            m_step, m_round = divmod(i + MULTIPLY_LAG, ROW_TILES)
+            prepare_m = m_step < K_STEPS and m_round < M_ROUNDS
+            if prepare_m:
+                regroup_m(m_step, m_round)
+            if 0 <= i - QUANTISE_LAG < N_CHUNKS:
+                quantise_x(i - QUANTISE_LAG)
+            if prepare_m:
+                quantise_m(m_step, m_round)
+            if 0 <= i < N_CHUNKS:
+                transpose_x(i)
+            if i >= MULTIPLY_LAG:
+                multiply(i - MULTIPLY_LAG)

@@ -16,21 +16,24 @@ LORA_GAIN = 2.0
 
 PACK = 4
 K_PASS = P * PACK
+PASS_WORDS = K_PASS // 2
 CHUNK_K = 4096
 PASSES = CHUNK_K // K_PASS
 K_STEPS = IN_F // CHUNK_K
 ROW_TILES = BATCH // P
 N_CHUNKS = K_STEPS * ROW_TILES
+LAST = N_CHUNKS - 1
 BANK_PASSES = 2
 CHUNK_BANKS = PASSES // BANK_PASSES
-QUANT_COLS = 2048
+BANK_K = BANK_PASSES * K_PASS
+ACC_TILES = 4
 
-LOADS_AHEAD = 6
-QUANTISE_LAG = 1
+LOADS_AHEAD = 8
 MULTIPLY_LAG = 2
+SORT_FROM = 4
 M_GROUP = 2
-M_ROUNDS = PASSES // M_GROUP
-VECTOR_BANK_EVERY = 8
+M_GROUPS = PASSES // M_GROUP
+LORA_ROUND = 5
 
 FLOPS = 2 * BATCH * IN_F * OUT_F + 2 * BATCH * RANK * OUT_F
 
@@ -42,10 +45,10 @@ def tile_lorasequential_pa_k_kernel(tc, x, h_lora, lora_B, M, out):
         const = ctx.enter_context(tc.tile_pool(name="const", bufs=1))
         x_pool = ctx.enter_context(tc.tile_pool(name="x", bufs=LOADS_AHEAD + 1))
         x_mx_pool = ctx.enter_context(tc.tile_pool(name="x_mx", bufs=3))
-        m_raw_pool = ctx.enter_context(tc.tile_pool(name="m_raw", bufs=2))
+        m_raw_pool = ctx.enter_context(tc.tile_pool(name="m_raw", bufs=2 * M_GROUPS))
         m_grouped_pool = ctx.enter_context(tc.tile_pool(name="m_grouped", bufs=3))
         m_mx_pool = ctx.enter_context(tc.tile_pool(name="m_mx", bufs=2))
-        result_pool = ctx.enter_context(tc.tile_pool(name="result", bufs=4))
+        result_pool = ctx.enter_context(tc.tile_pool(name="result", bufs=2))
         psum_t = ctx.enter_context(tc.psum_pool(name="psum_t", bufs=6))
         psum_acc = ctx.enter_context(tc.psum_pool(name="psum_acc", bufs=2))
 
@@ -55,6 +58,7 @@ def tile_lorasequential_pa_k_kernel(tc, x, h_lora, lora_B, M, out):
         make_identity(nc, ident_bf16[:])
 
         x_raw = {}
+        x_sorted = {}
         x_grouped = {}
         x_codes = {}
         x_scales = {}
@@ -62,38 +66,46 @@ def tile_lorasequential_pa_k_kernel(tc, x, h_lora, lora_B, M, out):
         m_grouped = {}
         m_codes = {}
         m_scales = {}
+        sums = [psum_acc.tile([P, ACC_TILES, OUT_F], F32, name="sums") for bank in range(ROW_TILES // ACC_TILES)]
 
-        def load_m(step):
-            raw = m_raw_pool.tile([P, PASSES, PACK, OUT_F], BF16, name="m_raw")
-            m_rows = M[step * CHUNK_K : (step + 1) * CHUNK_K, :]
-            nc.sync.dma_start(
-                out=raw[:],
-                in_=m_rows.rearrange("(g p t) o -> p g t o", p=P, t=PACK),
-            )
-            m_raw[step] = raw
+        first_width = (PASSES + ACC_TILES - 1) * OUT_F
+        m_codes[0] = const.tile([P, first_width], U32, name="m_codes_first", align_bytes=64)
+        m_scales[0] = const.tile([P, first_width], U8, name="m_scales_first", align_bytes=64)
+        nc.vector.memset(m_codes[0][:, PASSES * OUT_F :], 0)
+        nc.vector.memset(m_scales[0][:, PASSES * OUT_F :], 0)
+
+        def load_m(step, j):
+            raw = m_raw_pool.tile([P, M_GROUP, PACK, OUT_F], BF16, name="m_raw")
+            row = (step * PASSES + j * M_GROUP) * K_PASS
+            m_rows = M[row : row + M_GROUP * K_PASS, :]
+            nc.sync.dma_start(out=raw[:], in_=m_rows.rearrange("(g p t) o -> p g t o", p=P, t=PACK))
+            m_raw[step, j] = raw
+
+        def m_work(i):
+            if i < 2:
+                return [(0, 2 * i), (0, 2 * i + 1)]
+            step, k = divmod(i - 2, ROW_TILES)
+            return [(step + 1, k // 2)] if k % 2 == 0 and step + 1 < K_STEPS else []
 
         def load_x(chunk):
+            if chunk > 1:
+                for step, j in m_work(chunk):
+                    load_m(step, j)
             step, row_tile = divmod(chunk, ROW_TILES)
-            if row_tile == ROW_TILES - MULTIPLY_LAG and step + 1 < K_STEPS:
-                load_m(step + 1)
             raw = x_pool.tile([P, CHUNK_K], BF16, name="x_raw")
             x_rows = x[row_tile * P : (row_tile + 1) * P, step * CHUNK_K : (step + 1) * CHUNK_K]
-            pieces = CHUNK_BANKS if chunk == N_CHUNKS - 1 else 1
-            piece_k = CHUNK_K // pieces
+            piece_k = BANK_K if chunk in (0, LAST) else CHUNK_K
             for first in range(0, CHUNK_K, piece_k):
                 nc.sync.dma_start(out=raw[:, first : first + piece_k], in_=x_rows[:, first : first + piece_k])
             x_raw[chunk] = raw
 
         def regroup_m(step, j):
             grouped = m_grouped_pool.tile([P, M_GROUP, OUT_F, PACK], BF16, name="m_grouped", align_bytes=64)
-            nc.vector.tensor_copy(
-                out=grouped[:],
-                in_=m_raw[step][:, j * M_GROUP : (j + 1) * M_GROUP, :, :].rearrange("p g t o -> p g o t"),
-            )
+            nc.vector.tensor_copy(out=grouped[:], in_=m_raw[step, j][:].rearrange("p g t o -> p g o t"))
             m_grouped[step, j] = grouped
 
         def quantise_m(step, j):
-            if j == 0:
+            if step not in m_codes:
                 m_codes[step] = m_mx_pool.tile([P, PASSES * OUT_F], U32, name="m_codes", align_bytes=64)
                 m_scales[step] = m_mx_pool.tile([P, PASSES * OUT_F], U8, name="m_scales", align_bytes=64)
             cols = slice(j * M_GROUP * OUT_F, (j + 1) * M_GROUP * OUT_F)
@@ -103,6 +115,13 @@ def tile_lorasequential_pa_k_kernel(tc, x, h_lora, lora_B, M, out):
                 in_=m_grouped[step, j][:].rearrange("p g o t -> p (g o t)"),
             )
 
+        def sort_x(chunk):
+            passes = PASSES - SORT_FROM
+            ordered = x_mx_pool.tile([P, passes, 2, P], F32, name="x_sorted")
+            words = x_raw[chunk][:, SORT_FROM * K_PASS :].bitcast(F32)
+            nc.vector.tensor_copy(out=ordered[:], in_=words.rearrange("p (g w u) -> p g u w", g=passes, u=2))
+            x_sorted[chunk] = ordered
+
         def transpose_x(chunk):
             words = x_raw[chunk][:].bitcast(F32)
             grouped = x_mx_pool.tile([P, PASSES * P * PACK], BF16, name="x_grouped", align_bytes=64)
@@ -110,89 +129,133 @@ def tile_lorasequential_pa_k_kernel(tc, x, h_lora, lora_B, M, out):
             bank_words = BANK_PASSES * P * 2
             for bank in range(CHUNK_BANKS):
                 xt = psum_t.tile([P, BANK_PASSES, 2, P], F32, name="xt", tag="bank")
-                for g in range(BANK_PASSES):
-                    first = (bank * BANK_PASSES + g) * 2 * P
+                for j in range(BANK_PASSES):
+                    g = bank * BANK_PASSES + j
                     for u in range(2):
-                        nc.tensor.transpose(xt[:, g, u, :], words[:, first + u : first + 2 * P : 2], ident_f32[:])
+                        if chunk in x_sorted and g >= SORT_FROM:
+                            source = x_sorted[chunk][:, g - SORT_FROM, u, :]
+                        else:
+                            source = words[:, g * PASS_WORDS + u : (g + 1) * PASS_WORDS : 2]
+                        nc.tensor.transpose(xt[:, j, u, :], source, ident_f32[:])
                 side_by_side = grouped_words[:, bank * bank_words : (bank + 1) * bank_words].rearrange(
                     "p (g r u) -> p g r u", g=BANK_PASSES, u=2
                 )
-                if (chunk * CHUNK_BANKS + bank) % VECTOR_BANK_EVERY == VECTOR_BANK_EVERY - 1:
-                    nc.vector.tensor_copy(out=side_by_side, in_=xt[:].rearrange("p g u r -> p g r u"))
-                else:
-                    nc.scalar.copy(out=side_by_side, in_=xt[:].rearrange("p g u r -> p g r u"))
+                nc.scalar.copy(out=side_by_side, in_=xt[:].rearrange("p g u r -> p g r u"))
             x_grouped[chunk] = grouped
 
         def quantise_x(chunk):
             codes = x_mx_pool.tile([P, PASSES * P], U32, name="x_codes", align_bytes=64)
             scales = x_mx_pool.tile([P, PASSES * P], U8, name="x_scales", align_bytes=64)
-            for first in range(0, PASSES * P * PACK, QUANT_COLS):
-                cols = slice(first // PACK, (first + QUANT_COLS) // PACK)
+            quant_cols = (1 if chunk == LAST else 2) * BANK_PASSES * P * PACK
+            for first in range(0, PASSES * P * PACK, quant_cols):
+                cols = slice(first // PACK, (first + quant_cols) // PACK)
                 nc.vector.quantize_mx(
                     out=codes[:, cols].bitcast(FP8X4),
                     scales=scales[:, cols],
-                    in_=x_grouped[chunk][:, first : first + QUANT_COLS],
+                    in_=x_grouped[chunk][:, first : first + quant_cols],
                 )
             x_codes[chunk] = codes
             x_scales[chunk] = scales
 
         def multiply(chunk):
             step, row_tile = divmod(chunk, ROW_TILES)
-            acc = psum_acc.tile([P, OUT_F], F32, name="acc")
-            for g in range(PASSES):
+            bank, place = divmod(row_tile, ACC_TILES)
+            opens = step == 0 and place == 0
+            closes = step == K_STEPS - 1 and (row_tile == ACC_TILES - 1 or chunk == LAST - 1)
+            order = [PASSES - 1] + list(range(PASSES - 1)) if opens else list(range(PASSES))
+            if chunk == LAST:
+                last_sums.append(psum_t.tile([P, OUT_F], F32, name="last_sums", tag="bank"))
+            for g in order:
                 rows = slice(g * P, (g + 1) * P)
-                outputs = slice(g * OUT_F, (g + 1) * OUT_F)
+                wide = opens and g == order[0]
+                outputs = slice(g * OUT_F, (g + (ACC_TILES if wide else 1)) * OUT_F)
+                if chunk == LAST:
+                    target = last_sums[0][:]
+                elif wide:
+                    target = sums[bank][:].rearrange("p t o -> p (t o)")
+                else:
+                    target = sums[bank][:, place, :]
                 nc.tensor.matmul_mx(
-                    out=acc[:],
+                    out=target,
                     lhsT=x_codes[chunk][:, rows].bitcast(FP8X4),
                     lhsT_scale=x_scales[chunk][:, rows],
                     rhs=m_codes[step][:, outputs].bitcast(FP8X4),
                     rhs_scale=m_scales[step][:, outputs],
-                    start=(g == 0),
-                    stop=(g == PASSES - 1),
+                    start=wide or (chunk == LAST and g == order[0]),
+                    stop=(closes or chunk == LAST) and g == order[-1],
                 )
-            if step < K_STEPS - 1:
-                nc.vector.tensor_tensor(out=sums[:, row_tile, :], in0=acc[:], in1=sums[:, row_tile, :], op=ADD)
-            else:
-                result = result_pool.tile([P, OUT_F], F32, name="result")
-                nc.vector.tensor_tensor(out=result[:], in0=acc[:], in1=sums[:, row_tile, :], op=ADD)
-                nc.sync.dma_start(out=out[row_tile * P : (row_tile + 1) * P, :], in_=result[:])
 
+        def load_lora():
+            nc.sync.dma_start(out=h_sb[:], in_=h_lora.rearrange("g b r -> (g b) r").rearrange("(p j) r -> p j r", p=P))
+            nc.sync.dma_start(out=b_sb[:], in_=lora_B.rearrange("g r o -> r g o"))
+
+        def turn_h():
+            hT_ps = psum_t.tile([P, N_ADAPTERS, P], BF16, name="hT_ps", tag="bank")
+            for j in range(N_ADAPTERS):
+                nc.tensor.transpose(hT_ps[:, j, :], h_sb[:, j, :], ident_bf16[:])
+            nc.scalar.copy(out=hT_sb[:].rearrange("r (p j) -> r p j", p=P), in_=hT_ps[:].rearrange("r j p -> r p j"))
+
+        def make_lora():
+            for first in range(0, N_ADAPTERS, ACC_TILES):
+                y_ps = psum_t.tile([P, ACC_TILES, OUT_F], F32, name="y_ps", tag="bank")
+                for g in range(ACC_TILES):
+                    rows = slice((first + g) * P, (first + g + 1) * P)
+                    nc.tensor.matmul(
+                        y_ps[:, g, :], lhsT=hT_sb[:, rows], rhs=b_sb[:, first + g, :], start=True, stop=True
+                    )
+                nc.scalar.mul(out=lora[:, first : first + ACC_TILES, :], in_=y_ps[:], mul=LORA_GAIN)
+
+        def store(row_tile, result):
+            rows = out[row_tile * P : row_tile * P + result.shape[1] * P, :]
+            nc.sync.dma_start(out=rows.rearrange("(t p) o -> p t o", p=P), in_=result)
+
+        def add_lora(bank):
+            result = result_pool.tile([P, ACC_TILES, OUT_F], F32, name="result")
+            tiles = slice(bank * ACC_TILES, (bank + 1) * ACC_TILES)
+            nc.vector.tensor_tensor(out=result[:], in0=sums[bank][:], in1=lora[:, tiles, :], op=ADD)
+            return result
+
+        last_sums = []
         h_sb = const.tile([P, N_ADAPTERS, RANK], BF16)
-        nc.sync.dma_start(out=h_sb[:], in_=h_lora.rearrange("g b r -> b g r"))
         b_sb = const.tile([P, N_ADAPTERS, OUT_F], BF16)
-        nc.sync.dma_start(out=b_sb[:], in_=lora_B.rearrange("g r o -> r g o"))
-        load_m(0)
-        for chunk in range(LOADS_AHEAD):
+        hT_sb = const.tile([P, BATCH], BF16)
+        lora = const.tile([P, N_ADAPTERS, OUT_F], F32)
+
+        load_x(0)
+        load_m(0, 0)
+        load_m(0, 1)
+        load_x(1)
+        load_m(0, 2)
+        load_m(0, 3)
+        for chunk in range(2, LOADS_AHEAD):
             load_x(chunk)
+            if chunk == 3:
+                load_lora()
 
-        sums = const.tile([P, ROW_TILES, OUT_F], F32)
-        hT_ps = psum_t.tile([P, N_ADAPTERS, P], BF16, name="hT_ps", tag="bank")
-        for g in range(N_ADAPTERS):
-            nc.tensor.transpose(hT_ps[:, g, :], h_sb[:, g, :], ident_bf16[:])
-        hT_sb = const.tile([P, N_ADAPTERS, P], BF16)
-        nc.scalar.copy(out=hT_sb[:], in_=hT_ps[:])
-        bank_groups = 4
-        for first in range(0, N_ADAPTERS, bank_groups):
-            y_ps = psum_t.tile([P, bank_groups, OUT_F], F32, name="y_ps", tag="bank")
-            for g in range(bank_groups):
-                nc.tensor.matmul(
-                    y_ps[:, g, :], lhsT=hT_sb[:, first + g, :], rhs=b_sb[:, first + g, :], start=True, stop=True
-                )
-            nc.scalar.mul(out=sums[:, first : first + bank_groups, :], in_=y_ps[:], mul=LORA_GAIN)
-
-        for i in range(-MULTIPLY_LAG, N_CHUNKS + MULTIPLY_LAG):
-            if 0 <= i and i + LOADS_AHEAD < N_CHUNKS:
+        for i in range(N_CHUNKS + MULTIPLY_LAG):
+            if i + LOADS_AHEAD < N_CHUNKS:
                 load_x(i + LOADS_AHEAD)
-            m_step, m_round = divmod(i + MULTIPLY_LAG, ROW_TILES)
-            prepare_m = m_step < K_STEPS and m_round < M_ROUNDS
-            if prepare_m:
-                regroup_m(m_step, m_round)
-            if 0 <= i - QUANTISE_LAG < N_CHUNKS:
-                quantise_x(i - QUANTISE_LAG)
-            if prepare_m:
-                quantise_m(m_step, m_round)
-            if 0 <= i < N_CHUNKS:
+            for step, j in m_work(i):
+                regroup_m(step, j)
+            if 0 <= i - 1 < N_CHUNKS:
+                quantise_x(i - 1)
+            for step, j in m_work(i):
+                quantise_m(step, j)
+            if i + 1 < LAST:
+                sort_x(i + 1)
+            if i < N_CHUNKS:
                 transpose_x(i)
+            if i == LORA_ROUND:
+                turn_h()
+            if i == LORA_ROUND + 1:
+                make_lora()
             if i >= MULTIPLY_LAG:
                 multiply(i - MULTIPLY_LAG)
+            if i - MULTIPLY_LAG == N_CHUNKS - ACC_TILES - 1:
+                store(0, add_lora(0)[:])
+            if i - MULTIPLY_LAG == LAST - 1:
+                partial = add_lora(1)
+                store(ACC_TILES, partial[:, : ACC_TILES - 1, :])
+        result = result_pool.tile([P, 1, OUT_F], F32, name="last_result")
+        nc.vector.tensor_tensor(out=result[:, 0, :], in0=last_sums[0][:], in1=partial[:, ACC_TILES - 1, :], op=ADD)
+        store(ROW_TILES - 1, result[:])

from contextlib import ExitStack

import concourse.mybir as mybir
from concourse.masks import make_identity

BF16 = mybir.dt.bfloat16
F32 = mybir.dt.float32
U32 = mybir.dt.uint32
U8 = mybir.dt.uint8
FP8X4 = mybir.dt.float8_e4m3fn_x4
ADD = mybir.AluOpType.add

P = 128
BATCH, IN_F, OUT_F, RANK, N_ADAPTERS = 1024, 16384, 128, 128, 8
LORA_GAIN = 2.0

PACK = 4
K_PASS = P * PACK
PASS_WORDS = K_PASS // 2
CHUNK_K = 4096
PASSES = CHUNK_K // K_PASS
K_STEPS = IN_F // CHUNK_K
ROW_TILES = BATCH // P
N_CHUNKS = K_STEPS * ROW_TILES
LAST = N_CHUNKS - 1
BANK_PASSES = 2
CHUNK_BANKS = PASSES // BANK_PASSES
BANK_K = BANK_PASSES * K_PASS
ACC_TILES = 4

LOADS_AHEAD = 8
MULTIPLY_LAG = 2
SORT_FROM = 4
M_GROUP = 2
M_GROUPS = PASSES // M_GROUP
LORA_ROUND = 5

FLOPS = 2 * BATCH * IN_F * OUT_F + 2 * BATCH * RANK * OUT_F


def tile_lorasequential_pa_k_kernel(tc, x, h_lora, lora_B, M, out):
    nc = tc.nc
    with ExitStack() as ctx:
        ctx.enter_context(tc.manual_schedule())
        const = ctx.enter_context(tc.tile_pool(name="const", bufs=1))
        x_pool = ctx.enter_context(tc.tile_pool(name="x", bufs=LOADS_AHEAD + 1))
        x_mx_pool = ctx.enter_context(tc.tile_pool(name="x_mx", bufs=3))
        m_raw_pool = ctx.enter_context(tc.tile_pool(name="m_raw", bufs=2 * M_GROUPS))
        m_grouped_pool = ctx.enter_context(tc.tile_pool(name="m_grouped", bufs=3))
        m_mx_pool = ctx.enter_context(tc.tile_pool(name="m_mx", bufs=2))
        result_pool = ctx.enter_context(tc.tile_pool(name="result", bufs=2))
        psum_t = ctx.enter_context(tc.psum_pool(name="psum_t", bufs=6))
        psum_acc = ctx.enter_context(tc.psum_pool(name="psum_acc", bufs=2))

        ident_f32 = const.tile([P, P], F32)
        make_identity(nc, ident_f32[:])
        ident_bf16 = const.tile([P, P], BF16)
        make_identity(nc, ident_bf16[:])

        x_raw = {}
        x_sorted = {}
        x_grouped = {}
        x_codes = {}
        x_scales = {}
        m_raw = {}
        m_grouped = {}
        m_codes = {}
        m_scales = {}
        sums = [psum_acc.tile([P, ACC_TILES, OUT_F], F32, name="sums") for bank in range(ROW_TILES // ACC_TILES)]

        first_width = (PASSES + ACC_TILES - 1) * OUT_F
        m_codes[0] = const.tile([P, first_width], U32, name="m_codes_first", align_bytes=64)
        m_scales[0] = const.tile([P, first_width], U8, name="m_scales_first", align_bytes=64)
        nc.vector.memset(m_codes[0][:, PASSES * OUT_F :], 0)
        nc.vector.memset(m_scales[0][:, PASSES * OUT_F :], 0)

        def load_m(step, j):
            raw = m_raw_pool.tile([P, M_GROUP, PACK, OUT_F], BF16, name="m_raw")
            row = (step * PASSES + j * M_GROUP) * K_PASS
            m_rows = M[row : row + M_GROUP * K_PASS, :]
            nc.sync.dma_start(out=raw[:], in_=m_rows.rearrange("(g p t) o -> p g t o", p=P, t=PACK))
            m_raw[step, j] = raw

        def m_work(i):
            if i < 2:
                return [(0, 2 * i), (0, 2 * i + 1)]
            step, k = divmod(i - 2, ROW_TILES)
            return [(step + 1, k // 2)] if k % 2 == 0 and step + 1 < K_STEPS else []

        def load_x(chunk):
            if chunk > 1:
                for step, j in m_work(chunk):
                    load_m(step, j)
            step, row_tile = divmod(chunk, ROW_TILES)
            raw = x_pool.tile([P, CHUNK_K], BF16, name="x_raw")
            x_rows = x[row_tile * P : (row_tile + 1) * P, step * CHUNK_K : (step + 1) * CHUNK_K]
            piece_k = BANK_K if chunk in (0, LAST) else CHUNK_K
            for first in range(0, CHUNK_K, piece_k):
                nc.sync.dma_start(out=raw[:, first : first + piece_k], in_=x_rows[:, first : first + piece_k])
            x_raw[chunk] = raw

        def regroup_m(step, j):
            grouped = m_grouped_pool.tile([P, M_GROUP, OUT_F, PACK], BF16, name="m_grouped", align_bytes=64)
            nc.vector.tensor_copy(out=grouped[:], in_=m_raw[step, j][:].rearrange("p g t o -> p g o t"))
            m_grouped[step, j] = grouped

        def quantise_m(step, j):
            if step not in m_codes:
                m_codes[step] = m_mx_pool.tile([P, PASSES * OUT_F], U32, name="m_codes", align_bytes=64)
                m_scales[step] = m_mx_pool.tile([P, PASSES * OUT_F], U8, name="m_scales", align_bytes=64)
            cols = slice(j * M_GROUP * OUT_F, (j + 1) * M_GROUP * OUT_F)
            nc.vector.quantize_mx(
                out=m_codes[step][:, cols].bitcast(FP8X4),
                scales=m_scales[step][:, cols],
                in_=m_grouped[step, j][:].rearrange("p g o t -> p (g o t)"),
            )

        def sort_x(chunk):
            passes = PASSES - SORT_FROM
            ordered = x_mx_pool.tile([P, passes, 2, P], F32, name="x_sorted")
            words = x_raw[chunk][:, SORT_FROM * K_PASS :].bitcast(F32)
            nc.vector.tensor_copy(out=ordered[:], in_=words.rearrange("p (g w u) -> p g u w", g=passes, u=2))
            x_sorted[chunk] = ordered

        def transpose_x(chunk):
            words = x_raw[chunk][:].bitcast(F32)
            grouped = x_mx_pool.tile([P, PASSES * P * PACK], BF16, name="x_grouped", align_bytes=64)
            grouped_words = grouped[:].bitcast(F32)
            bank_words = BANK_PASSES * P * 2
            for bank in range(CHUNK_BANKS):
                xt = psum_t.tile([P, BANK_PASSES, 2, P], F32, name="xt", tag="bank")
                for j in range(BANK_PASSES):
                    g = bank * BANK_PASSES + j
                    for u in range(2):
                        if chunk in x_sorted and g >= SORT_FROM:
                            source = x_sorted[chunk][:, g - SORT_FROM, u, :]
                        else:
                            source = words[:, g * PASS_WORDS + u : (g + 1) * PASS_WORDS : 2]
                        nc.tensor.transpose(xt[:, j, u, :], source, ident_f32[:])
                side_by_side = grouped_words[:, bank * bank_words : (bank + 1) * bank_words].rearrange(
                    "p (g r u) -> p g r u", g=BANK_PASSES, u=2
                )
                nc.scalar.copy(out=side_by_side, in_=xt[:].rearrange("p g u r -> p g r u"))
            x_grouped[chunk] = grouped

        def quantise_x(chunk):
            codes = x_mx_pool.tile([P, PASSES * P], U32, name="x_codes", align_bytes=64)
            scales = x_mx_pool.tile([P, PASSES * P], U8, name="x_scales", align_bytes=64)
            quant_cols = (1 if chunk == LAST else 2) * BANK_PASSES * P * PACK
            for first in range(0, PASSES * P * PACK, quant_cols):
                cols = slice(first // PACK, (first + quant_cols) // PACK)
                nc.vector.quantize_mx(
                    out=codes[:, cols].bitcast(FP8X4),
                    scales=scales[:, cols],
                    in_=x_grouped[chunk][:, first : first + quant_cols],
                )
            x_codes[chunk] = codes
            x_scales[chunk] = scales

        def multiply(chunk):
            step, row_tile = divmod(chunk, ROW_TILES)
            bank, place = divmod(row_tile, ACC_TILES)
            opens = step == 0 and place == 0
            closes = step == K_STEPS - 1 and (row_tile == ACC_TILES - 1 or chunk == LAST - 1)
            order = [PASSES - 1] + list(range(PASSES - 1)) if opens else list(range(PASSES))
            if chunk == LAST:
                last_sums.append(psum_t.tile([P, OUT_F], F32, name="last_sums", tag="bank"))
            for g in order:
                rows = slice(g * P, (g + 1) * P)
                wide = opens and g == order[0]
                outputs = slice(g * OUT_F, (g + (ACC_TILES if wide else 1)) * OUT_F)
                if chunk == LAST:
                    target = last_sums[0][:]
                elif wide:
                    target = sums[bank][:].rearrange("p t o -> p (t o)")
                else:
                    target = sums[bank][:, place, :]
                nc.tensor.matmul_mx(
                    out=target,
                    lhsT=x_codes[chunk][:, rows].bitcast(FP8X4),
                    lhsT_scale=x_scales[chunk][:, rows],
                    rhs=m_codes[step][:, outputs].bitcast(FP8X4),
                    rhs_scale=m_scales[step][:, outputs],
                    start=wide or (chunk == LAST and g == order[0]),
                    stop=(closes or chunk == LAST) and g == order[-1],
                )

        def load_lora():
            nc.sync.dma_start(out=h_sb[:], in_=h_lora.rearrange("g b r -> (g b) r").rearrange("(p j) r -> p j r", p=P))
            nc.sync.dma_start(out=b_sb[:], in_=lora_B.rearrange("g r o -> r g o"))

        def turn_h():
            hT_ps = psum_t.tile([P, N_ADAPTERS, P], BF16, name="hT_ps", tag="bank")
            for j in range(N_ADAPTERS):
                nc.tensor.transpose(hT_ps[:, j, :], h_sb[:, j, :], ident_bf16[:])
            nc.scalar.copy(out=hT_sb[:].rearrange("r (p j) -> r p j", p=P), in_=hT_ps[:].rearrange("r j p -> r p j"))

        def make_lora():
            for first in range(0, N_ADAPTERS, ACC_TILES):
                y_ps = psum_t.tile([P, ACC_TILES, OUT_F], F32, name="y_ps", tag="bank")
                for g in range(ACC_TILES):
                    rows = slice((first + g) * P, (first + g + 1) * P)
                    nc.tensor.matmul(
                        y_ps[:, g, :], lhsT=hT_sb[:, rows], rhs=b_sb[:, first + g, :], start=True, stop=True
                    )
                nc.scalar.mul(out=lora[:, first : first + ACC_TILES, :], in_=y_ps[:], mul=LORA_GAIN)

        def store(row_tile, result):
            rows = out[row_tile * P : row_tile * P + result.shape[1] * P, :]
            nc.sync.dma_start(out=rows.rearrange("(t p) o -> p t o", p=P), in_=result)

        def add_lora(bank):
            result = result_pool.tile([P, ACC_TILES, OUT_F], F32, name="result")
            tiles = slice(bank * ACC_TILES, (bank + 1) * ACC_TILES)
            nc.vector.tensor_tensor(out=result[:], in0=sums[bank][:], in1=lora[:, tiles, :], op=ADD)
            return result

        last_sums = []
        h_sb = const.tile([P, N_ADAPTERS, RANK], BF16)
        b_sb = const.tile([P, N_ADAPTERS, OUT_F], BF16)
        hT_sb = const.tile([P, BATCH], BF16)
        lora = const.tile([P, N_ADAPTERS, OUT_F], F32)

        load_x(0)
        load_m(0, 0)
        load_m(0, 1)
        load_x(1)
        load_m(0, 2)
        load_m(0, 3)
        for chunk in range(2, LOADS_AHEAD):
            load_x(chunk)
            if chunk == 3:
                load_lora()

        for i in range(N_CHUNKS + MULTIPLY_LAG):
            if i + LOADS_AHEAD < N_CHUNKS:
                load_x(i + LOADS_AHEAD)
            for step, j in m_work(i):
                regroup_m(step, j)
            if 0 <= i - 1 < N_CHUNKS:
                quantise_x(i - 1)
            for step, j in m_work(i):
                quantise_m(step, j)
            if i + 1 < LAST:
                sort_x(i + 1)
            if i < N_CHUNKS:
                transpose_x(i)
            if i == LORA_ROUND:
                turn_h()
            if i == LORA_ROUND + 1:
                make_lora()
            if i >= MULTIPLY_LAG:
                multiply(i - MULTIPLY_LAG)
            if i - MULTIPLY_LAG == N_CHUNKS - ACC_TILES - 1:
                store(0, add_lora(0)[:])
            if i - MULTIPLY_LAG == LAST - 1:
                partial = add_lora(1)
                store(ACC_TILES, partial[:, : ACC_TILES - 1, :])
        result = result_pool.tile([P, 1, OUT_F], F32, name="last_result")
        nc.vector.tensor_tensor(out=result[:, 0, :], in0=last_sums[0][:], in1=partial[:, ACC_TILES - 1, :], op=ADD)
        store(ROW_TILES - 1, result[:])
